import numpy as np
import ml_dtypes

BF16 = ml_dtypes.bfloat16


def bf(x):
    return np.asarray(x, np.float32).astype(BF16)


def f32(x):
    return np.asarray(x, np.float32)


def f64(x):
    return np.asarray(x).astype(np.float64)


def striped(idx):
    return np.tile(idx.reshape(-1, 16).T, (8, 1))


C, S, N = 512, 1024, 512


def positional():
    pos = np.arange(N, dtype=np.float32)[None, :]
    ch = np.arange(C, dtype=np.float32)[:, None]
    angle = pos / np.power(np.float32(10000.0), np.float32(2.0) * ch / np.float32(C))
    return np.where(np.arange(C)[:, None] % 2 == 0, np.sin(f64(angle)), np.cos(f64(angle)))


def setup_inputs():
    return {"table": f32(np.random.standard_normal((C, S))), "pe": f32(positional()), "offs": striped(np.random.permutation(np.tile(np.arange(S), 2))[:N])}


def reference(table, pe, offs):
    idx = offs[:16].T.reshape(-1)
    return f64(table)[:, idx] + f64(pe)

@@ -1,0 +1,34 @@
+import concourse.mybir as mybir
+
+F32 = mybir.dt.float32
+U16 = mybir.dt.uint16
+ADD = mybir.AluOpType.add
+
+P = 128
+
+
+def tile_transformer_kernel(tc, table, pe, offs, out):
+    nc = tc.nc
+    features, words = table.shape
+    tokens = pe.shape[1]
+    blocks = features // P
+
+    table_blocks = table.rearrange("(b p) v -> b p v", p=P)
+    pe_blocks = pe.rearrange("(b p) j -> b p j", p=P)
+    out_blocks = out.rearrange("(b p) j -> b p j", p=P)
+
+    with (
+        tc.tile_pool(name="held", bufs=1) as held,
+        tc.tile_pool(name="work", bufs=blocks) as work,
+    ):
+        offsets = held.tile([P, tokens // 16], U16, name="offsets")
+        nc.sync.dma_start(offsets[:], offs)
+
+        for b in range(blocks):
+            window = work.tile([P, words], F32, name="window")
+            place = work.tile([P, tokens], F32, name="place")
+            summed = work.tile([P, tokens], F32, name="summed")
+            nc.sync.dma_start(window[:], table_blocks[b])
+            nc.scalar.dma_start(place[:], pe_blocks[b])
+            nc.vector.tensor_tensor(summed[:], window[:].indirect(offsets[:]), place[:], ADD)
+            nc.scalar.dma_start(out_blocks[b], summed[:])

@@ -17,18 +17,21 @@ def tile_transformer_kernel(tc, table, pe, offs, out):
     pe_blocks = pe.rearrange("(b p) j -> b p j", p=P)
     out_blocks = out.rearrange("(b p) j -> b p j", p=P)
 
-    with (
-        tc.tile_pool(name="held", bufs=1) as held,
-        tc.tile_pool(name="work", bufs=blocks) as work,
-    ):
+    with tc.tile_pool(name="held", bufs=1) as held:
         offsets = held.tile([P, tokens // 16], U16, name="offsets")
         nc.sync.dma_start(offsets[:], offs)
 
+        windows = []
+        places = []
         for b in range(blocks):
-            window = work.tile([P, words], F32, name="window")
-            place = work.tile([P, tokens], F32, name="place")
-            summed = work.tile([P, tokens], F32, name="summed")
+            window = held.tile([P, words], F32, name=f"window{b}")
+            place = held.tile([P, tokens], F32, name=f"place{b}")
             nc.sync.dma_start(window[:], table_blocks[b])
-            nc.scalar.dma_start(place[:], pe_blocks[b])
-            nc.vector.tensor_tensor(summed[:], window[:].indirect(offsets[:]), place[:], ADD)
-            nc.scalar.dma_start(out_blocks[b], summed[:])
+            nc.sync.dma_start(place[:], pe_blocks[b])
+            windows.append(window)
+            places.append(place)
+
+        for b in range(blocks):
+            summed = held.tile([P, tokens], F32, name=f"summed{b}")
+            nc.vector.tensor_tensor(summed[:], windows[b][:].indirect(offsets[:]), places[b][:], ADD)
+            nc.sync.dma_start(out_blocks[b], summed[:])

@@ -6,6 +6,8 @@ ADD = mybir.AluOpType.add
 
 P = 128
 
+LAST_PIECES = 4
+
 
 def tile_transformer_kernel(tc, table, pe, offs, out):
     nc = tc.nc
@@ -17,6 +19,10 @@ def tile_transformer_kernel(tc, table, pe, offs, out):
     pe_blocks = pe.rearrange("(b p) j -> b p j", p=P)
     out_blocks = out.rearrange("(b p) j -> b p j", p=P)
 
+    def token_pieces(b):
+        width = tokens // LAST_PIECES if b == blocks - 1 else tokens
+        return [(lo, lo + width) for lo in range(0, tokens, width)]
+
     with tc.tile_pool(name="held", bufs=1) as held:
         offsets = held.tile([P, tokens // 16], U16, name="offsets")
         nc.sync.dma_start(offsets[:], offs)
@@ -27,11 +33,14 @@ def tile_transformer_kernel(tc, table, pe, offs, out):
             window = held.tile([P, words], F32, name=f"window{b}")
             place = held.tile([P, tokens], F32, name=f"place{b}")
             nc.sync.dma_start(window[:], table_blocks[b])
-            nc.sync.dma_start(place[:], pe_blocks[b])
+            for lo, hi in token_pieces(b):
+                nc.sync.dma_start(place[:, lo:hi], pe_blocks[b][:, lo:hi])
             windows.append(window)
             places.append(place)
 
         for b in range(blocks):
             summed = held.tile([P, tokens], F32, name=f"summed{b}")
-            nc.vector.tensor_tensor(summed[:], windows[b][:].indirect(offsets[:]), places[b][:], ADD)
-            nc.sync.dma_start(out_blocks[b], summed[:])
+            for lo, hi in token_pieces(b):
+                picked = windows[b][:].indirect(offsets[:, lo // 16 : hi // 16])
+                nc.vector.tensor_tensor(summed[:, lo:hi], picked, places[b][:, lo:hi], ADD)
+                nc.sync.dma_start(out_blocks[b][:, lo:hi], summed[:, lo:hi])

@@ -6,7 +6,7 @@ ADD = mybir.AluOpType.add
 
 P = 128
 
-LAST_PIECES = 4
+LAST_PIECES = 2
 
 
 def tile_transformer_kernel(tc, table, pe, offs, out):

@@ -32,7 +32,8 @@ def tile_transformer_kernel(tc, table, pe, offs, out):
         for b in range(blocks):
             window = held.tile([P, words], F32, name=f"window{b}")
             place = held.tile([P, tokens], F32, name=f"place{b}")
-            nc.sync.dma_start(window[:], table_blocks[b])
+            first_or_sync = nc.scalar if b == 0 else nc.sync
+            first_or_sync.dma_start(window[:], table_blocks[b])
             for lo, hi in token_pieces(b):
                 nc.sync.dma_start(place[:, lo:hi], pe_blocks[b][:, lo:hi])
             windows.append(window)

@@ -25,7 +25,6 @@ def tile_transformer_kernel(tc, table, pe, offs, out):
 
     with tc.tile_pool(name="held", bufs=1) as held:
         offsets = held.tile([P, tokens // 16], U16, name="offsets")
-        nc.sync.dma_start(offsets[:], offs)
 
         windows = []
         places = []
@@ -36,6 +35,8 @@ def tile_transformer_kernel(tc, table, pe, offs, out):
             first_or_sync.dma_start(window[:], table_blocks[b])
             for lo, hi in token_pieces(b):
                 nc.sync.dma_start(place[:, lo:hi], pe_blocks[b][:, lo:hi])
+            if b == 0:
+                nc.sync.dma_start(offsets[:], offs)
             windows.append(window)
             places.append(place)
 

@@ -6,6 +6,8 @@ ADD = mybir.AluOpType.add
 
 P = 128
 
+ROW_ALIGN = 256
+
 LAST_PIECES = 2
 
 
@@ -29,8 +31,8 @@ def tile_transformer_kernel(tc, table, pe, offs, out):
         windows = []
         places = []
         for b in range(blocks):
-            window = held.tile([P, words], F32, name=f"window{b}")
-            place = held.tile([P, tokens], F32, name=f"place{b}")
+            window = held.tile([P, words], F32, name=f"window{b}", align_bytes=ROW_ALIGN)
+            place = held.tile([P, tokens], F32, name=f"place{b}", align_bytes=ROW_ALIGN)
             first_or_sync = nc.scalar if b == 0 else nc.sync
             first_or_sync.dma_start(window[:], table_blocks[b])
             for lo, hi in token_pieces(b):
@@ -41,7 +43,7 @@ def tile_transformer_kernel(tc, table, pe, offs, out):
             places.append(place)
 
         for b in range(blocks):
-            summed = held.tile([P, tokens], F32, name=f"summed{b}")
+            summed = held.tile([P, tokens], F32, name=f"summed{b}", align_bytes=ROW_ALIGN)
             for lo, hi in token_pieces(b):
                 picked = windows[b][:].indirect(offsets[:, lo // 16 : hi // 16])
                 nc.vector.tensor_tensor(summed[:, lo:hi], picked, places[b][:, lo:hi], ADD)

@@ -8,8 +8,6 @@ P = 128
 
 ROW_ALIGN = 256
 
-LAST_PIECES = 2
-
 
 def tile_transformer_kernel(tc, table, pe, offs, out):
     nc = tc.nc
@@ -17,34 +15,57 @@ def tile_transformer_kernel(tc, table, pe, offs, out):
     tokens = pe.shape[1]
     blocks = features // P
 
-    table_blocks = table.rearrange("(b p) v -> b p v", p=P)
-    pe_blocks = pe.rearrange("(b p) j -> b p j", p=P)
-    out_blocks = out.rearrange("(b p) j -> b p j", p=P)
-
-    def token_pieces(b):
-        width = tokens // LAST_PIECES if b == blocks - 1 else tokens
-        return [(lo, lo + width) for lo in range(0, tokens, width)]
+    table_blocks = table.rearrange("(p b) v -> b p v", b=blocks)
+    pe_rows = pe.rearrange("(p b) j -> p (b j)", b=blocks)
+    out_rows = out.rearrange("(p b) j -> p (b j)", b=blocks)
 
     with tc.tile_pool(name="held", bufs=1) as held:
-        offsets = held.tile([P, tokens // 16], U16, name="offsets")
+        offsets = held.tile([P, tokens // 16], U16, name="offsets", align_bytes=ROW_ALIGN)
+        places = held.tile([P, blocks * tokens], F32, name="places", align_bytes=ROW_ALIGN)
+        sums = held.tile([P, blocks * tokens], F32, name="sums", align_bytes=ROW_ALIGN)
+        windows = [
+            held.tile([P, words], F32, name=f"window{b}", align_bytes=ROW_ALIGN)
+            for b in range(blocks)
+        ]
 
-        windows = []
-        places = []
-        for b in range(blocks):
-            window = held.tile([P, words], F32, name=f"window{b}", align_bytes=ROW_ALIGN)
-            place = held.tile([P, tokens], F32, name=f"place{b}", align_bytes=ROW_ALIGN)
-            first_or_sync = nc.scalar if b == 0 else nc.sync
-            first_or_sync.dma_start(window[:], table_blocks[b])
-            for lo, hi in token_pieces(b):
-                nc.sync.dma_start(place[:, lo:hi], pe_blocks[b][:, lo:hi])
-            if b == 0:
-                nc.sync.dma_start(offsets[:], offs)
-            windows.append(window)
-            places.append(place)
+        def load_window(b, engine):
+            engine.dma_start(windows[b][:], table_blocks[b])
 
-        for b in range(blocks):
-            summed = held.tile([P, tokens], F32, name=f"summed{b}", align_bytes=ROW_ALIGN)
-            for lo, hi in token_pieces(b):
-                picked = windows[b][:].indirect(offsets[:, lo // 16 : hi // 16])
-                nc.vector.tensor_tensor(summed[:, lo:hi], picked, places[b][:, lo:hi], ADD)
-                nc.sync.dma_start(out_blocks[b][:, lo:hi], summed[:, lo:hi])
+        def load_places(lo, hi):
+            nc.sync.dma_start(places[:, lo:hi], pe_rows[:, lo:hi])
+
+        def store_sums(lo, hi):
+            nc.sync.dma_start(out_rows[:, lo:hi], sums[:, lo:hi])
+
+        def look_up_and_add(b, lo, hi):
+            columns = slice(b * tokens + lo, b * tokens + hi)
+            picked = windows[b][:].indirect(offsets[:, lo // 16 : hi // 16])
+            nc.vector.tensor_tensor(sums[:, columns], picked, places[:, columns], ADD)
+
+        last = blocks - 1
+        start = last * tokens
+        quarter, half = tokens // 4, tokens // 2
+
+        load_window(0, nc.scalar)
+        load_places(0, tokens)
+        nc.sync.dma_start(offsets[:], offs)
+        load_window(1, nc.sync)
+        load_places(tokens, 2 * tokens + half)
+        load_window(2, nc.sync)
+        load_places(2 * tokens + half, start + quarter)
+        load_window(last, nc.sync)
+        load_places(start + quarter, start + half)
+        load_places(start + half, start + tokens)
+
+        look_up_and_add(0, 0, tokens)
+        store_sums(0, tokens)
+        look_up_and_add(1, 0, tokens)
+        store_sums(tokens, 2 * tokens)
+        look_up_and_add(2, 0, half)
+        look_up_and_add(2, half, tokens)
+        store_sums(2 * tokens, start)
+        look_up_and_add(last, 0, quarter)
+        look_up_and_add(last, quarter, half)
+        store_sums(start, start + half)
+        look_up_and_add(last, half, tokens)
+        store_sums(start + half, start + tokens)

@@ -58,14 +58,14 @@ def tile_transformer_kernel(tc, table, pe, offs, out):
         load_places(start + half, start + tokens)
 
         look_up_and_add(0, 0, tokens)
-        store_sums(0, tokens)
         look_up_and_add(1, 0, tokens)
-        store_sums(tokens, 2 * tokens)
+        store_sums(0, 2 * tokens)
         look_up_and_add(2, 0, half)
         look_up_and_add(2, half, tokens)
         store_sums(2 * tokens, start)
         look_up_and_add(last, 0, quarter)
         look_up_and_add(last, quarter, half)
         store_sums(start, start + half)
-        look_up_and_add(last, half, tokens)
-        store_sums(start + half, start + tokens)
+        for lo in (half, half + quarter):
+            look_up_and_add(last, lo, lo + quarter)
+            store_sums(start + lo, start + lo + quarter)

import concourse.mybir as mybir

F32 = mybir.dt.float32
U16 = mybir.dt.uint16
ADD = mybir.AluOpType.add

P = 128

ROW_ALIGN = 256


def tile_transformer_kernel(tc, table, pe, offs, out):
    nc = tc.nc
    features, words = table.shape
    tokens = pe.shape[1]
    blocks = features // P

    table_blocks = table.rearrange("(p b) v -> b p v", b=blocks)
    pe_rows = pe.rearrange("(p b) j -> p (b j)", b=blocks)
    out_rows = out.rearrange("(p b) j -> p (b j)", b=blocks)

    with tc.tile_pool(name="held", bufs=1) as held:
        offsets = held.tile([P, tokens // 16], U16, name="offsets", align_bytes=ROW_ALIGN)
        places = held.tile([P, blocks * tokens], F32, name="places", align_bytes=ROW_ALIGN)
        sums = held.tile([P, blocks * tokens], F32, name="sums", align_bytes=ROW_ALIGN)
        windows = [
            held.tile([P, words], F32, name=f"window{b}", align_bytes=ROW_ALIGN)
            for b in range(blocks)
        ]

        def load_window(b, engine):
            engine.dma_start(windows[b][:], table_blocks[b])

        def load_places(lo, hi):
            nc.sync.dma_start(places[:, lo:hi], pe_rows[:, lo:hi])

        def store_sums(lo, hi):
            nc.sync.dma_start(out_rows[:, lo:hi], sums[:, lo:hi])

        def look_up_and_add(b, lo, hi):
            columns = slice(b * tokens + lo, b * tokens + hi)
            picked = windows[b][:].indirect(offsets[:, lo // 16 : hi // 16])
            nc.vector.tensor_tensor(sums[:, columns], picked, places[:, columns], ADD)

        last = blocks - 1
        start = last * tokens
        quarter, half = tokens // 4, tokens // 2

        load_window(0, nc.scalar)
        load_places(0, tokens)
        nc.sync.dma_start(offsets[:], offs)
        load_window(1, nc.sync)
        load_places(tokens, 2 * tokens + half)
        load_window(2, nc.sync)
        load_places(2 * tokens + half, start + quarter)
        load_window(last, nc.sync)
        load_places(start + quarter, start + half)
        load_places(start + half, start + tokens)

        look_up_and_add(0, 0, tokens)
        look_up_and_add(1, 0, tokens)
        store_sums(0, 2 * tokens)
        look_up_and_add(2, 0, half)
        look_up_and_add(2, half, tokens)
        store_sums(2 * tokens, start)
        look_up_and_add(last, 0, quarter)
        look_up_and_add(last, quarter, half)
        store_sums(start, start + half)
        for lo in (half, half + quarter):
            look_up_and_add(last, lo, lo + quarter)
            store_sums(start + lo, start + lo + quarter)
